import numpy as np
import ml_dtypes


def mxq(x, axis, fmt="e4m3"):
    dtype, down = {"e4m3": (ml_dtypes.float8_e4m3fn, 7), "e5m2": (ml_dtypes.float8_e5m2, 14)}[fmt]
    v = np.moveaxis(np.asarray(x, np.float32).astype(ml_dtypes.bfloat16).astype(np.float64), axis, -1)
    blocks = v.reshape(v.shape[:-1] + (-1, 32))
    amax = np.abs(blocks).max(-1, keepdims=True)
    byte = np.maximum(np.where(amax > 0, np.frexp(amax)[1] - 1 + 127, 0) - down, 1)
    scale = np.exp2(byte - 127.0)
    codes = (blocks / scale).astype(np.float32).astype(dtype).astype(np.float64)
    return np.moveaxis((codes * scale).reshape(v.shape), -1, axis)


WIDE = False


def mx_kscale(k):
    if not WIDE:
        return np.ones(k)
    levels = np.array([10, -10, 5, -5, 0])
    a = np.random.permutation(np.resize(levels, k // 512 * 4)).reshape(k // 512, 4)
    idx = np.arange(k)
    return np.exp2(a[idx // 512, idx % 128 // 32])


BF16 = ml_dtypes.bfloat16


def bf(x):
    return np.asarray(x, np.float32).astype(BF16)


def f64(x):
    return np.asarray(x).astype(np.float64)


B, T, C, HS, DW, DA, DV, DG = 4, 1024, 1024, 64, 128, 128, 128, 256


def sigmoid(z):
    return 1.0 / (1.0 + np.exp(-z))


def setup_inputs():
    s = mx_kscale(C)
    return {
        "x": bf(np.random.standard_normal((B, T, C)) * s),
        "v_first": bf(np.random.standard_normal((B, T, C))),
        "x_v": bf(np.random.uniform(0.0, 1.0, C)),
        "Wv": bf(np.random.standard_normal((C, C)) / np.sqrt(C) / s[None, :]),
        "v0": bf(np.random.standard_normal(C)),
        "xv_v1": bf(0.8 * np.random.standard_normal((B, T, DV))),
        "v2": bf(np.random.standard_normal((DV, C)) / np.sqrt(DV)),
    }


def reference(x, v_first, x_v, Wv, v0, xv_v1, v2):
    x = f64(x)
    xprev = np.concatenate([np.zeros_like(x[:, :1]), x[:, :-1]], axis=1)
    xx = xprev - x
    xv = x + xx * f64(x_v)
    v = mxq(xv, 2, "e4m3") @ mxq(f64(Wv), 1, "e4m3").T
    v = v + (f64(v_first) - v) * sigmoid(f64(v0) + f64(xv_v1) @ f64(v2))
    return v

@@ -1,0 +1,329 @@
+from contextlib import ExitStack
+
+import concourse.mybir as mybir
+from concourse.masks import make_identity
+
+F32 = mybir.dt.float32
+BF16 = mybir.dt.bfloat16
+U32 = mybir.dt.uint32
+U8 = mybir.dt.uint8
+FP8X4 = mybir.dt.float8_e4m3fn_x4
+ALU = mybir.AluOpType
+ACT = mybir.ActivationFunctionType
+
+P = 128
+TOK = 4096
+C = 1024
+DV = 128
+CHUNK = 512
+NCHUNK = TOK // CHUNK
+NT = TOK // P
+SEQ_CHUNKS = 1024 // CHUNK
+PAD = 8
+TW = PAD + CHUNK
+HALF = CHUNK // 2
+
+FLOPS = 2 * TOK * C * C + 2 * TOK * DV * C
+
+
+def tile_full_tmix_params_pb_t_kernel(tc, x, v_first, x_v, Wv, v0, xv_v1, v2, out):
+    nc = tc.nc
+    xf = x.flatten_outer_dims()
+    vff = v_first.flatten_outer_dims()
+    af = xv_v1.flatten_outer_dims()
+    of = out.flatten_outer_dims()
+
+    with ExitStack() as ctx:
+        ctx.enter_context(tc.manual_schedule())
+        const = ctx.enter_context(tc.tile_pool(name="const", bufs=1))
+        wpool = ctx.enter_context(tc.tile_pool(name="wpool", bufs=1))
+        xpool = ctx.enter_context(tc.tile_pool(name="xpool", bufs=3))
+        vpool = ctx.enter_context(tc.tile_pool(name="vpool", bufs=3))
+        t1pool = ctx.enter_context(tc.tile_pool(name="t1pool", bufs=3))
+        t2pool = ctx.enter_context(tc.tile_pool(name="t2pool", bufs=3))
+        gpool = ctx.enter_context(tc.tile_pool(name="gpool", bufs=2))
+        cpool = ctx.enter_context(tc.tile_pool(name="cpool", bufs=4))
+        spool = ctx.enter_context(tc.tile_pool(name="spool", bufs=3))
+        dpool = ctx.enter_context(tc.tile_pool(name="dpool", bufs=5))
+        psA = ctx.enter_context(tc.psum_pool(name="psA", bufs=2))
+        psP = ctx.enter_context(tc.psum_pool(name="psP", bufs=4))
+        psZ = ctx.enter_context(tc.psum_pool(name="psZ", bufs=2))
+
+        xs_tiles = {}
+        vf_tiles = {}
+        xt_tiles = {}
+        t1_tiles = {}
+        t2_tiles = {}
+        grp_tiles = {}
+        xc_tiles = {}
+        xsc_tiles = {}
+        pp_tiles = {}
+        zz_tiles = {}
+        gs_tiles = {}
+        d_tiles = {}
+
+        def load_x(ck):
+            xs = xpool.tile([P, 4, C], BF16, name="xs")
+            nc.sync.dma_start(
+                out=xs[:],
+                in_=xf[CHUNK * ck : CHUNK * (ck + 1), :].rearrange("(t p) c -> p t c", p=P),
+            )
+            xs_tiles[ck] = xs
+
+        def load_vf(ck):
+            vt = vpool.tile([P, 4, C], BF16, name="vt")
+            nc.sync.dma_start(
+                out=vt[:],
+                in_=vff[CHUNK * ck : CHUNK * (ck + 1), :].rearrange("(t p) c -> p t c", p=P),
+            )
+            vf_tiles[ck] = vt
+
+        wrow = const.tile([P, 2 * P], BF16, name="wrow")
+        nc.vector.memset(wrow[:], 0.0)
+        nc.sync.dma_start(out=wrow[0:4, :], in_=x_v.rearrange("(u q) -> u q", q=2 * P))
+        load_x(0)
+        wv_sb = wpool.tile([P, 8, C], BF16, name="wv_sb")
+        wv_view = Wv.rearrange("(o p) k -> p o k", p=P)
+        for q in range(4):
+            nc.sync.dma_start(out=wv_sb[:, 2 * q : 2 * q + 2, :], in_=wv_view[:, 2 * q : 2 * q + 2, :])
+        a_sb = const.tile([P, NT, DV], BF16, name="a_sb")
+        nc.sync.dma_start(out=a_sb[:], in_=af.rearrange("(m p) d -> p m d", p=P))
+        v0row = const.tile([P, P], BF16, name="v0row")
+        nc.vector.memset(v0row[:], 0.0)
+        nc.sync.dma_start(out=v0row[0:8, :], in_=v0.rearrange("(o p) -> o p", p=P))
+        v0one = const.tile([P, 512], BF16, name="v0one")
+        nc.vector.memset(v0one[:], 0.0)
+        nc.sync.dma_start(out=v0one[0:1, :], in_=v0.rearrange("(o c) -> o c", c=512)[0:1, :])
+        v2_sb = const.tile([P, C], BF16, name="v2_sb")
+        nc.sync.dma_start(out=v2_sb[:], in_=v2)
+        load_x(1)
+        load_vf(0)
+
+        ident_f = const.tile([P, P], F32, name="ident_f")
+        make_identity(nc, ident_f[:])
+        ident_b = const.tile([P, P], BF16, name="ident_b")
+        make_identity(nc, ident_b[:])
+        ones_b = const.tile([P, P], BF16, name="ones_b")
+        nc.vector.memset(ones_b[:], 1.0)
+
+        wps = psZ.tile([P, 512], F32, name="wps", tag="zz")
+        nc.tensor.transpose(wps[:, 0:P], wrow[:].bitcast(F32), ident_f[:])
+        w_col = const.tile([P, 8], F32, name="w_col")
+        nc.vector.tensor_copy(out=w_col[:], in_=wps[:].bitcast(BF16)[:, 0:8])
+        omw = const.tile([P, 8], F32, name="omw")
+        nc.vector.tensor_scalar(
+            out=omw[:], in0=w_col[:], scalar1=-1.0, scalar2=1.0, op0=ALU.mult, op1=ALU.add
+        )
+        v0T = const.tile([P, 4, P], F32, name="v0T")
+        aT = const.tile([P, TOK], BF16, name="aT")
+
+        def prep_v0():
+            v0ps = psZ.tile([P, P], BF16, name="v0ps", tag="zz")
+            nc.tensor.transpose(v0ps[:], v0row[:], ident_b[:])
+            nc.vector.tensor_copy(out=v0T[:], in_=v0ps[:, 4:8].unsqueeze(2).to_broadcast([P, 4, P]))
+
+        def prep_aT(k):
+            aps = psP.tile([P, 1024], BF16, name="aps", tag="pp")
+            for m in range(8):
+                nc.tensor.transpose(aps[:, P * m : P * (m + 1)], a_sb[:, 8 * k + m, :], ident_b[:])
+            nc.vector.tensor_copy(out=aT[:, 1024 * k : 1024 * (k + 1)], in_=aps[:])
+
+        w_codes = const.tile([P, 2, C], U32, name="w_codes", align_bytes=64)
+        w_scales = const.tile([P, 2, C], U8, name="w_scales", align_bytes=64)
+        wg0 = wpool.tile([P, 4 * C], BF16, name="wg0", align_bytes=64)
+        wg1 = wpool.tile([P, 4 * C], BF16, name="wg1", align_bytes=64)
+        wgs = [wg0, wg1]
+
+        def prep_w(q):
+            for g in range(2):
+                wt = psP.tile([P, 2, 256], F32, name="wt", tag="pp")
+                for u in range(2):
+                    for oo in range(2):
+                        i = 2 * g + u
+                        nc.tensor.transpose(
+                            wt[:, u, P * oo : P * (oo + 1)],
+                            wv_sb[:, 2 * q + oo, :].bitcast(F32)[:, P * i : P * (i + 1)],
+                            ident_f[:],
+                        )
+                nc.vector.tensor_copy(
+                    out=wgs[g][:, 1024 * q : 1024 * (q + 1)].bitcast(F32).rearrange("p (c u) -> p c u", u=2),
+                    in_=wt[:].rearrange("p u c -> p c u"),
+                )
+            if q % 2 == 1:
+                h = q // 2
+                for g in range(2):
+                    nc.vector.quantize_mx(
+                        out=w_codes[:, g, 512 * h : 512 * (h + 1)].bitcast(FP8X4),
+                        scales=w_scales[:, g, 512 * h : 512 * (h + 1)],
+                        in_=wgs[g][:, 2048 * h : 2048 * (h + 1)],
+                    )
+
+        def xtr(a):
+            ck, i = divmod(a, 4)
+            xs = xs_tiles[ck]
+            xt = psA.tile([P, CHUNK], F32, name="xt")
+            for tt in range(4):
+                nc.tensor.transpose(
+                    xt[:, P * tt : P * (tt + 1)],
+                    xs[:, tt, :].bitcast(F32)[:, P * i : P * (i + 1)],
+                    ident_f[:],
+                )
+            xt_tiles[a] = xt
+
+        def tops(a):
+            ck, i = divmod(a, 4)
+            g, u = divmod(i, 2)
+            if u == 0:
+                t1 = t1pool.tile([P, 4, CHUNK], F32, name="t1")
+                t2 = t2pool.tile([P, 4, TW], F32, name="t2")
+                t1_tiles[(ck, g)] = t1
+                t2_tiles[(ck, g)] = t2
+                if ck % SEQ_CHUNKS == 0:
+                    nc.gpsimd.memset(t2[:, :, PAD - 1 : PAD], 0.0)
+                else:
+                    nc.gpsimd.tensor_copy(
+                        out=t2[:, :, PAD - 1 : PAD], in_=t2_tiles[(ck - 1, g)][:, :, TW - 1 : TW]
+                    )
+            t1 = t1_tiles[(ck, g)]
+            t2 = t2_tiles[(ck, g)]
+            xb = xt_tiles[a][:].bitcast(BF16).rearrange("p (t e) -> p t e", e=2)
+            for e in range(2):
+                j = 2 * u + e
+                pl = 4 * g + j
+                nc.scalar.activation(
+                    out=t1[:, j, :], in_=xb[:, :, e], func=ACT.Copy, scale=omw[:, pl : pl + 1]
+                )
+                nc.scalar.activation(
+                    out=t2[:, j, PAD:TW], in_=xb[:, :, e], func=ACT.Copy, scale=w_col[:, pl : pl + 1]
+                )
+
+        def addh(r):
+            ck, rr = divmod(r, 4)
+            g, hh = divmod(rr, 2)
+            if hh == 0:
+                grp = gpool.tile([P, CHUNK, 4], BF16, name="grp", align_bytes=64)
+                grp_tiles[(ck, g)] = grp
+            grp = grp_tiles[(ck, g)]
+            t1 = t1_tiles[(ck, g)]
+            t2 = t2_tiles[(ck, g)]
+            lo = HALF * hh
+            nc.vector.tensor_tensor(
+                out=grp[:, lo : lo + HALF, :],
+                in0=t1[:, :, lo : lo + HALF].rearrange("p j t -> p t j"),
+                in1=t2[:, :, PAD - 1 + lo : PAD - 1 + lo + HALF].rearrange("p j t -> p t j"),
+                op=ALU.add,
+            )
+
+        def quanth(r):
+            ck, rr = divmod(r, 4)
+            g, hh = divmod(rr, 2)
+            if hh == 0:
+                xc = cpool.tile([P, CHUNK], U32, name="xc", align_bytes=64)
+                xsc = cpool.tile([P, CHUNK], U8, name="xsc", align_bytes=64)
+                xc_tiles[(ck, g)] = xc
+                xsc_tiles[(ck, g)] = xsc
+            lo = HALF * hh
+            nc.vector.quantize_mx(
+                out=xc_tiles[(ck, g)][:, lo : lo + HALF].bitcast(FP8X4),
+                scales=xsc_tiles[(ck, g)][:, lo : lo + HALF],
+                in_=grp_tiles[(ck, g)][:, lo : lo + HALF, :].rearrange("p t j -> p (t j)"),
+            )
+
+        def mx(n):
+            ck, tt = divmod(n, 4)
+            ts = slice(P * tt, P * (tt + 1))
+            for h in range(2):
+                cs = slice(512 * h, 512 * (h + 1))
+                pp = psP.tile([P, 512], F32, name="pp")
+                pp_tiles[(n, h)] = pp
+                for g in range(2):
+                    nc.tensor.matmul_mx(
+                        out=pp[:],
+                        lhsT=xc_tiles[(ck, g)][:, ts].bitcast(FP8X4),
+                        lhsT_scale=xsc_tiles[(ck, g)][:, ts],
+                        rhs=w_codes[:, g, cs].bitcast(FP8X4),
+                        rhs_scale=w_scales[:, g, cs],
+                        start=(g == 0),
+                        stop=(g == 1),
+                    )
+
+        def zgrp(n):
+            for h in range(2):
+                cs = slice(512 * h, 512 * (h + 1))
+                zz = psZ.tile([P, 512], F32, name="zz")
+                zz_tiles[(n, h)] = zz
+                if h == 0:
+                    nc.tensor.matmul(out=zz[:], lhsT=ones_b[:], rhs=v0one[:], start=True, stop=False)
+                else:
+                    for i in range(4):
+                        nc.tensor.matmul(
+                            out=zz[:, P * i : P * (i + 1)],
+                            lhsT=v0T[:, i, :],
+                            rhs=ident_f[:],
+                            is_transpose=True,
+                            start=(i == 0),
+                            stop=False,
+                        )
+                nc.tensor.matmul(
+                    out=zz[:], lhsT=aT[:, P * n : P * (n + 1)], rhs=v2_sb[:, cs], start=False, stop=True
+                )
+
+        def sig(n):
+            gs = spool.tile([P, C], F32, name="gs")
+            gs_tiles[n] = gs
+            for h in range(2):
+                nc.scalar.activation(
+                    out=gs[:, 512 * h : 512 * (h + 1)], in_=zz_tiles[(n, h)][:], func=ACT.Sigmoid
+                )
+
+        def v1(n):
+            ck, tt = divmod(n, 4)
+            d = dpool.tile([P, C], F32, name="d")
+            d_tiles[n] = d
+            for h in range(2):
+                cs = slice(512 * h, 512 * (h + 1))
+                nc.vector.tensor_tensor(
+                    out=d[:, cs], in0=vf_tiles[ck][:, tt, cs], in1=pp_tiles[(n, h)][:], op=ALU.subtract
+                )
+
+        def v2op(n):
+            d = d_tiles[n]
+            nc.gpsimd.tensor_tensor(out=d[:], in0=d[:], in1=gs_tiles[n][:], op=ALU.mult)
+
+        def fin(n):
+            d = d_tiles[n]
+            for h in range(2):
+                cs = slice(512 * h, 512 * (h + 1))
+                nc.vector.tensor_tensor(out=d[:, cs], in0=d[:, cs], in1=pp_tiles[(n, h)][:], op=ALU.add)
+            nc.sync.dma_start(out=of[P * n : P * (n + 1), :], in_=d[:])
+
+        for n in range(-8, NT + 1):
+            if 0 <= n - 1 < NT:
+                fin(n - 1)
+            if (n + 14) % 4 == 0 and 2 <= (n + 14) // 4 < NCHUNK:
+                load_x((n + 14) // 4)
+            if (n + 7) % 4 == 0 and 1 <= (n + 7) // 4 < NCHUNK:
+                load_vf((n + 7) // 4)
+            if 0 <= n + 1 < NT:
+                mx(n + 1)
+                sig(n + 1)
+            if 0 <= n + 7 < NT:
+                tops(n + 7)
+            if 0 <= n + 2 < NT:
+                zgrp(n + 2)
+            if 0 <= n + 8 < NT:
+                xtr(n + 8)
+            if -6 <= n <= -3:
+                prep_w(n + 6)
+            if n == -3:
+                prep_v0()
+                for k in range(4):
+                    prep_aT(k)
+            if 0 <= n + 5 < NT:
+                addh(n + 5)
+            if 0 <= n + 1 < NT:
+                v1(n + 1)
+            if 0 <= n + 5 < NT:
+                quanth(n + 5)
+            if 0 <= n + 1 < NT:
+                v2op(n + 1)

@@ -19,8 +19,7 @@ CHUNK = 512
 NCHUNK = TOK // CHUNK
 NT = TOK // P
 SEQ_CHUNKS = 1024 // CHUNK
-PAD = 8
-TW = PAD + CHUNK
+TW = CHUNK + 4
 HALF = CHUNK // 2
 
 FLOPS = 2 * TOK * C * C + 2 * TOK * DV * C
@@ -87,7 +86,8 @@ def tile_full_tmix_params_pb_t_kernel(tc, x, v_first, x_v, Wv, v0, xv_v1, v2, ou
         for q in range(4):
             nc.sync.dma_start(out=wv_sb[:, 2 * q : 2 * q + 2, :], in_=wv_view[:, 2 * q : 2 * q + 2, :])
         a_sb = const.tile([P, NT, DV], BF16, name="a_sb")
-        nc.sync.dma_start(out=a_sb[:], in_=af.rearrange("(m p) d -> p m d", p=P))
+        a_view = af.rearrange("(m p) d -> p m d", p=P)
+        nc.sync.dma_start(out=a_sb[:, 0:8, :], in_=a_view[:, 0:8, :])
         v0row = const.tile([P, P], BF16, name="v0row")
         nc.vector.memset(v0row[:], 0.0)
         nc.sync.dma_start(out=v0row[0:8, :], in_=v0.rearrange("(o p) -> o p", p=P))
@@ -98,6 +98,8 @@ def tile_full_tmix_params_pb_t_kernel(tc, x, v_first, x_v, Wv, v0, xv_v1, v2, ou
         nc.sync.dma_start(out=v2_sb[:], in_=v2)
         load_x(1)
         load_vf(0)
+        nc.sync.dma_start(out=a_sb[:, 8:NT, :], in_=a_view[:, 8:NT, :])
+        load_x(2)
 
         ident_f = const.tile([P, P], F32, name="ident_f")
         make_identity(nc, ident_f[:])
@@ -105,6 +107,8 @@ def tile_full_tmix_params_pb_t_kernel(tc, x, v_first, x_v, Wv, v0, xv_v1, v2, ou
         make_identity(nc, ident_b[:])
         ones_b = const.tile([P, P], BF16, name="ones_b")
         nc.vector.memset(ones_b[:], 1.0)
+        zero4 = const.tile([P, 4], F32, name="zero4")
+        nc.vector.memset(zero4[:], 0.0)
 
         wps = psZ.tile([P, 512], F32, name="wps", tag="zz")
         nc.tensor.transpose(wps[:, 0:P], wrow[:].bitcast(F32), ident_f[:])
@@ -179,10 +183,10 @@ def tile_full_tmix_params_pb_t_kernel(tc, x, v_first, x_v, Wv, v0, xv_v1, v2, ou
                 t1_tiles[(ck, g)] = t1
                 t2_tiles[(ck, g)] = t2
                 if ck % SEQ_CHUNKS == 0:
-                    nc.gpsimd.memset(t2[:, :, PAD - 1 : PAD], 0.0)
+                    nc.scalar.copy(out=t2[:, :, 0:1], in_=zero4[:].unsqueeze(2))
                 else:
-                    nc.gpsimd.tensor_copy(
-                        out=t2[:, :, PAD - 1 : PAD], in_=t2_tiles[(ck - 1, g)][:, :, TW - 1 : TW]
+                    nc.scalar.copy(
+                        out=t2[:, :, 0:1], in_=t2_tiles[(ck - 1, g)][:, :, CHUNK : CHUNK + 1]
                     )
             t1 = t1_tiles[(ck, g)]
             t2 = t2_tiles[(ck, g)]
@@ -194,7 +198,7 @@ def tile_full_tmix_params_pb_t_kernel(tc, x, v_first, x_v, Wv, v0, xv_v1, v2, ou
                     out=t1[:, j, :], in_=xb[:, :, e], func=ACT.Copy, scale=omw[:, pl : pl + 1]
                 )
                 nc.scalar.activation(
-                    out=t2[:, j, PAD:TW], in_=xb[:, :, e], func=ACT.Copy, scale=w_col[:, pl : pl + 1]
+                    out=t2[:, j, 1 : CHUNK + 1], in_=xb[:, :, e], func=ACT.Copy, scale=w_col[:, pl : pl + 1]
                 )
 
         def addh(r):
@@ -208,9 +212,9 @@ def tile_full_tmix_params_pb_t_kernel(tc, x, v_first, x_v, Wv, v0, xv_v1, v2, ou
             t2 = t2_tiles[(ck, g)]
             lo = HALF * hh
             nc.vector.tensor_tensor(
-                out=grp[:, lo : lo + HALF, :],
-                in0=t1[:, :, lo : lo + HALF].rearrange("p j t -> p t j"),
-                in1=t2[:, :, PAD - 1 + lo : PAD - 1 + lo + HALF].rearrange("p j t -> p t j"),
+                out=grp[:, lo : lo + HALF, :].rearrange("p (c i) j -> p c j i", i=4),
+                in0=t1[:, :, lo : lo + HALF].rearrange("p j (c i) -> p c j i", i=4),
+                in1=t2[:, :, lo : lo + HALF].rearrange("p j (c i) -> p c j i", i=4),
                 op=ALU.add,
             )
 
@@ -297,33 +301,35 @@ def tile_full_tmix_params_pb_t_kernel(tc, x, v_first, x_v, Wv, v0, xv_v1, v2, ou
                 nc.vector.tensor_tensor(out=d[:, cs], in0=d[:, cs], in1=pp_tiles[(n, h)][:], op=ALU.add)
             nc.sync.dma_start(out=of[P * n : P * (n + 1), :], in_=d[:])
 
-        for n in range(-8, NT + 1):
+        for n in range(-9, NT + 1):
             if 0 <= n - 1 < NT:
                 fin(n - 1)
-            if (n + 14) % 4 == 0 and 2 <= (n + 14) // 4 < NCHUNK:
-                load_x((n + 14) // 4)
-            if (n + 7) % 4 == 0 and 1 <= (n + 7) // 4 < NCHUNK:
-                load_vf((n + 7) // 4)
+            if (n + 17) % 4 == 0 and 3 <= (n + 17) // 4 < NCHUNK:
+                load_x((n + 17) // 4)
+            if (n + 9) % 4 == 0 and 1 <= (n + 9) // 4 < NCHUNK:
+                load_vf((n + 9) // 4)
             if 0 <= n + 1 < NT:
                 mx(n + 1)
                 sig(n + 1)
-            if 0 <= n + 7 < NT:
-                tops(n + 7)
+            if 0 <= n + 8 < NT:
+                tops(n + 8)
             if 0 <= n + 2 < NT:
                 zgrp(n + 2)
-            if 0 <= n + 8 < NT:
-                xtr(n + 8)
-            if -6 <= n <= -3:
-                prep_w(n + 6)
-            if n == -3:
-                prep_v0()
-                for k in range(4):
-                    prep_aT(k)
-            if 0 <= n + 5 < NT:
-                addh(n + 5)
+            if 0 <= n + 9 < NT:
+                xtr(n + 9)
+            if -7 <= n <= -4:
+                prep_w(n + 7)
             if 0 <= n + 1 < NT:
                 v1(n + 1)
             if 0 <= n + 5 < NT:
                 quanth(n + 5)
+            if 0 <= n + 6 < NT:
+                addh(n + 6)
+            if n == -5:
+                prep_v0()
+                prep_aT(0)
+            if n == -2:
+                for k in range(1, 4):
+                    prep_aT(k)
             if 0 <= n + 1 < NT:
                 v2op(n + 1)

@@ -38,7 +38,7 @@ def tile_full_tmix_params_pb_t_kernel(tc, x, v_first, x_v, Wv, v0, xv_v1, v2, ou
         wpool = ctx.enter_context(tc.tile_pool(name="wpool", bufs=1))
         xpool = ctx.enter_context(tc.tile_pool(name="xpool", bufs=3))
         vpool = ctx.enter_context(tc.tile_pool(name="vpool", bufs=3))
-        t1pool = ctx.enter_context(tc.tile_pool(name="t1pool", bufs=3))
+        xvpool = ctx.enter_context(tc.tile_pool(name="xvpool", bufs=3))
         t2pool = ctx.enter_context(tc.tile_pool(name="t2pool", bufs=3))
         gpool = ctx.enter_context(tc.tile_pool(name="gpool", bufs=2))
         cpool = ctx.enter_context(tc.tile_pool(name="cpool", bufs=4))
@@ -51,7 +51,7 @@ def tile_full_tmix_params_pb_t_kernel(tc, x, v_first, x_v, Wv, v0, xv_v1, v2, ou
         xs_tiles = {}
         vf_tiles = {}
         xt_tiles = {}
-        t1_tiles = {}
+        xvp_tiles = {}
         t2_tiles = {}
         grp_tiles = {}
         xc_tiles = {}
@@ -130,7 +130,7 @@ def tile_full_tmix_params_pb_t_kernel(tc, x, v_first, x_v, Wv, v0, xv_v1, v2, ou
             aps = psP.tile([P, 1024], BF16, name="aps", tag="pp")
             for m in range(8):
                 nc.tensor.transpose(aps[:, P * m : P * (m + 1)], a_sb[:, 8 * k + m, :], ident_b[:])
-            nc.vector.tensor_copy(out=aT[:, 1024 * k : 1024 * (k + 1)], in_=aps[:])
+            nc.scalar.copy(out=aT[:, 1024 * k : 1024 * (k + 1)], in_=aps[:])
 
         w_codes = const.tile([P, 2, C], U32, name="w_codes", align_bytes=64)
         w_scales = const.tile([P, 2, C], U8, name="w_scales", align_bytes=64)
@@ -149,10 +149,11 @@ def tile_full_tmix_params_pb_t_kernel(tc, x, v_first, x_v, Wv, v0, xv_v1, v2, ou
                             wv_sb[:, 2 * q + oo, :].bitcast(F32)[:, P * i : P * (i + 1)],
                             ident_f[:],
                         )
-                nc.vector.tensor_copy(
-                    out=wgs[g][:, 1024 * q : 1024 * (q + 1)].bitcast(F32).rearrange("p (c u) -> p c u", u=2),
-                    in_=wt[:].rearrange("p u c -> p c u"),
-                )
+                w_dst = wgs[g][:, 1024 * q : 1024 * (q + 1)].bitcast(F32).rearrange("p (c u) -> p c u", u=2)
+                if g == 0:
+                    nc.vector.tensor_copy(out=w_dst, in_=wt[:].rearrange("p u c -> p c u"))
+                else:
+                    nc.scalar.copy(out=w_dst, in_=wt[:].rearrange("p u c -> p c u"))
             if q % 2 == 1:
                 h = q // 2
                 for g in range(2):
@@ -174,13 +175,11 @@ def tile_full_tmix_params_pb_t_kernel(tc, x, v_first, x_v, Wv, v0, xv_v1, v2, ou
                 )
             xt_tiles[a] = xt
 
-        def tops(a):
+        def t2ops(a):
             ck, i = divmod(a, 4)
             g, u = divmod(i, 2)
             if u == 0:
-                t1 = t1pool.tile([P, 4, CHUNK], F32, name="t1")
                 t2 = t2pool.tile([P, 4, TW], F32, name="t2")
-                t1_tiles[(ck, g)] = t1
                 t2_tiles[(ck, g)] = t2
                 if ck % SEQ_CHUNKS == 0:
                     nc.scalar.copy(out=t2[:, :, 0:1], in_=zero4[:].unsqueeze(2))
@@ -188,34 +187,48 @@ def tile_full_tmix_params_pb_t_kernel(tc, x, v_first, x_v, Wv, v0, xv_v1, v2, ou
                     nc.scalar.copy(
                         out=t2[:, :, 0:1], in_=t2_tiles[(ck - 1, g)][:, :, CHUNK : CHUNK + 1]
                     )
-            t1 = t1_tiles[(ck, g)]
             t2 = t2_tiles[(ck, g)]
             xb = xt_tiles[a][:].bitcast(BF16).rearrange("p (t e) -> p t e", e=2)
             for e in range(2):
                 j = 2 * u + e
                 pl = 4 * g + j
                 nc.scalar.activation(
-                    out=t1[:, j, :], in_=xb[:, :, e], func=ACT.Copy, scale=omw[:, pl : pl + 1]
-                )
-                nc.scalar.activation(
                     out=t2[:, j, 1 : CHUNK + 1], in_=xb[:, :, e], func=ACT.Copy, scale=w_col[:, pl : pl + 1]
                 )
 
-        def addh(r):
+        def a2ops(a):
+            ck, i = divmod(a, 4)
+            g, u = divmod(i, 2)
+            if u == 0:
+                xvp = xvpool.tile([P, 4, CHUNK], BF16, name="xvp")
+                xvp_tiles[(ck, g)] = xvp
+            xvp = xvp_tiles[(ck, g)]
+            t2 = t2_tiles[(ck, g)]
+            xb = xt_tiles[a][:].bitcast(BF16).rearrange("p (t e) -> p t e", e=2)
+            for e in range(2):
+                j = 2 * u + e
+                pl = 4 * g + j
+                nc.vector.scalar_tensor_tensor(
+                    out=xvp[:, j, :],
+                    in0=xb[:, :, e],
+                    scalar=omw[:, pl : pl + 1],
+                    in1=t2[:, j, 0:CHUNK],
+                    op0=ALU.mult,
+                    op1=ALU.add,
+                )
+
+        def rg(r):
             ck, rr = divmod(r, 4)
             g, hh = divmod(rr, 2)
             if hh == 0:
                 grp = gpool.tile([P, CHUNK, 4], BF16, name="grp", align_bytes=64)
                 grp_tiles[(ck, g)] = grp
             grp = grp_tiles[(ck, g)]
-            t1 = t1_tiles[(ck, g)]
-            t2 = t2_tiles[(ck, g)]
+            xvp = xvp_tiles[(ck, g)]
             lo = HALF * hh
-            nc.vector.tensor_tensor(
+            nc.scalar.copy(
                 out=grp[:, lo : lo + HALF, :].rearrange("p (c i) j -> p c j i", i=4),
-                in0=t1[:, :, lo : lo + HALF].rearrange("p j (c i) -> p c j i", i=4),
-                in1=t2[:, :, lo : lo + HALF].rearrange("p j (c i) -> p c j i", i=4),
-                op=ALU.add,
+                in_=xvp[:, :, lo : lo + HALF].rearrange("p j (c i) -> p c j i", i=4),
             )
 
         def quanth(r):
@@ -301,30 +314,32 @@ def tile_full_tmix_params_pb_t_kernel(tc, x, v_first, x_v, Wv, v0, xv_v1, v2, ou
                 nc.vector.tensor_tensor(out=d[:, cs], in0=d[:, cs], in1=pp_tiles[(n, h)][:], op=ALU.add)
             nc.sync.dma_start(out=of[P * n : P * (n + 1), :], in_=d[:])
 
-        for n in range(-9, NT + 1):
+        for n in range(-10, NT + 1):
             if 0 <= n - 1 < NT:
                 fin(n - 1)
-            if (n + 17) % 4 == 0 and 3 <= (n + 17) // 4 < NCHUNK:
-                load_x((n + 17) // 4)
+            if (n + 18) % 4 == 0 and 3 <= (n + 18) // 4 < NCHUNK:
+                load_x((n + 18) // 4)
             if (n + 9) % 4 == 0 and 1 <= (n + 9) // 4 < NCHUNK:
                 load_vf((n + 9) // 4)
             if 0 <= n + 1 < NT:
                 mx(n + 1)
                 sig(n + 1)
-            if 0 <= n + 8 < NT:
-                tops(n + 8)
+            if 0 <= n + 9 < NT:
+                t2ops(n + 9)
+            if 0 <= n + 6 < NT:
+                rg(n + 6)
             if 0 <= n + 2 < NT:
                 zgrp(n + 2)
-            if 0 <= n + 9 < NT:
-                xtr(n + 9)
-            if -7 <= n <= -4:
-                prep_w(n + 7)
+            if -8 <= n <= -5:
+                prep_w(n + 8)
+            if 0 <= n + 10 < NT:
+                xtr(n + 10)
+            if 0 <= n + 8 < NT:
+                a2ops(n + 8)
             if 0 <= n + 1 < NT:
                 v1(n + 1)
             if 0 <= n + 5 < NT:
                 quanth(n + 5)
-            if 0 <= n + 6 < NT:
-                addh(n + 6)
             if n == -5:
                 prep_v0()
                 prep_aT(0)

@@ -44,6 +44,7 @@ def tile_full_tmix_params_pb_t_kernel(tc, x, v_first, x_v, Wv, v0, xv_v1, v2, ou
         cpool = ctx.enter_context(tc.tile_pool(name="cpool", bufs=4))
         spool = ctx.enter_context(tc.tile_pool(name="spool", bufs=3))
         dpool = ctx.enter_context(tc.tile_pool(name="dpool", bufs=5))
+        apool = ctx.enter_context(tc.tile_pool(name="apool", bufs=2))
         psA = ctx.enter_context(tc.psum_pool(name="psA", bufs=2))
         psP = ctx.enter_context(tc.psum_pool(name="psP", bufs=4))
         psZ = ctx.enter_context(tc.psum_pool(name="psZ", bufs=2))
@@ -60,13 +61,14 @@ def tile_full_tmix_params_pb_t_kernel(tc, x, v_first, x_v, Wv, v0, xv_v1, v2, ou
         zz_tiles = {}
         gs_tiles = {}
         d_tiles = {}
+        aT_tiles = {}
 
-        def load_x(ck):
+        def load_x(ck, pieces):
             xs = xpool.tile([P, 4, C], BF16, name="xs")
-            nc.sync.dma_start(
-                out=xs[:],
-                in_=xf[CHUNK * ck : CHUNK * (ck + 1), :].rearrange("(t p) c -> p t c", p=P),
-            )
+            src = xf[CHUNK * ck : CHUNK * (ck + 1), :].rearrange("(t p) c -> p t c", p=P)
+            w = C // pieces
+            for i in range(pieces):
+                nc.sync.dma_start(out=xs[:, :, w * i : w * (i + 1)], in_=src[:, :, w * i : w * (i + 1)])
             xs_tiles[ck] = xs
 
         def load_vf(ck):
@@ -80,7 +82,7 @@ def tile_full_tmix_params_pb_t_kernel(tc, x, v_first, x_v, Wv, v0, xv_v1, v2, ou
         wrow = const.tile([P, 2 * P], BF16, name="wrow")
         nc.vector.memset(wrow[:], 0.0)
         nc.sync.dma_start(out=wrow[0:4, :], in_=x_v.rearrange("(u q) -> u q", q=2 * P))
-        load_x(0)
+        load_x(0, 4)
         wv_sb = wpool.tile([P, 8, C], BF16, name="wv_sb")
         wv_view = Wv.rearrange("(o p) k -> p o k", p=P)
         for q in range(4):
@@ -96,10 +98,10 @@ def tile_full_tmix_params_pb_t_kernel(tc, x, v_first, x_v, Wv, v0, xv_v1, v2, ou
         nc.sync.dma_start(out=v0one[0:1, :], in_=v0.rearrange("(o c) -> o c", c=512)[0:1, :])
         v2_sb = const.tile([P, C], BF16, name="v2_sb")
         nc.sync.dma_start(out=v2_sb[:], in_=v2)
-        load_x(1)
+        load_x(1, 1)
         load_vf(0)
         nc.sync.dma_start(out=a_sb[:, 8:NT, :], in_=a_view[:, 8:NT, :])
-        load_x(2)
+        load_x(2, 1)
 
         ident_f = const.tile([P, P], F32, name="ident_f")
         make_identity(nc, ident_f[:])
@@ -119,18 +121,19 @@ def tile_full_tmix_params_pb_t_kernel(tc, x, v_first, x_v, Wv, v0, xv_v1, v2, ou
             out=omw[:], in0=w_col[:], scalar1=-1.0, scalar2=1.0, op0=ALU.mult, op1=ALU.add
         )
         v0T = const.tile([P, 4, P], F32, name="v0T")
-        aT = const.tile([P, TOK], BF16, name="aT")
 
         def prep_v0():
             v0ps = psZ.tile([P, P], BF16, name="v0ps", tag="zz")
             nc.tensor.transpose(v0ps[:], v0row[:], ident_b[:])
             nc.vector.tensor_copy(out=v0T[:], in_=v0ps[:, 4:8].unsqueeze(2).to_broadcast([P, 4, P]))
 
-        def prep_aT(k):
-            aps = psP.tile([P, 1024], BF16, name="aps", tag="pp")
-            for m in range(8):
-                nc.tensor.transpose(aps[:, P * m : P * (m + 1)], a_sb[:, 8 * k + m, :], ident_b[:])
-            nc.scalar.copy(out=aT[:, 1024 * k : 1024 * (k + 1)], in_=aps[:])
+        def prep_aT(ck):
+            aps = psZ.tile([P, CHUNK], BF16, name="aps", tag="zz")
+            for m in range(4):
+                nc.tensor.transpose(aps[:, P * m : P * (m + 1)], a_sb[:, 4 * ck + m, :], ident_b[:])
+            aT = apool.tile([P, CHUNK], BF16, name="aT")
+            nc.scalar.copy(out=aT[:], in_=aps[:])
+            aT_tiles[ck] = aT
 
         w_codes = const.tile([P, 2, C], U32, name="w_codes", align_bytes=64)
         w_scales = const.tile([P, 2, C], U8, name="w_scales", align_bytes=64)
@@ -154,8 +157,9 @@ def tile_full_tmix_params_pb_t_kernel(tc, x, v_first, x_v, Wv, v0, xv_v1, v2, ou
                     nc.vector.tensor_copy(out=w_dst, in_=wt[:].rearrange("p u c -> p c u"))
                 else:
                     nc.scalar.copy(out=w_dst, in_=wt[:].rearrange("p u c -> p c u"))
-            if q % 2 == 1:
-                h = q // 2
+
+        def quant_w(h):
+            if True:
                 for g in range(2):
                     nc.vector.quantize_mx(
                         out=w_codes[:, g, 512 * h : 512 * (h + 1)].bitcast(FP8X4),
@@ -265,7 +269,8 @@ def tile_full_tmix_params_pb_t_kernel(tc, x, v_first, x_v, Wv, v0, xv_v1, v2, ou
                     )
 
         def zgrp(n):
-            for h in range(2):
+            ck, tt = divmod(n, 4)
+            for h in (1, 0):
                 cs = slice(512 * h, 512 * (h + 1))
                 zz = psZ.tile([P, 512], F32, name="zz")
                 zz_tiles[(n, h)] = zz
@@ -282,13 +287,13 @@ def tile_full_tmix_params_pb_t_kernel(tc, x, v_first, x_v, Wv, v0, xv_v1, v2, ou
                             stop=False,
                         )
                 nc.tensor.matmul(
-                    out=zz[:], lhsT=aT[:, P * n : P * (n + 1)], rhs=v2_sb[:, cs], start=False, stop=True
+                    out=zz[:], lhsT=aT_tiles[ck][:, P * tt : P * (tt + 1)], rhs=v2_sb[:, cs], start=False, stop=True
                 )
 
         def sig(n):
             gs = spool.tile([P, C], F32, name="gs")
             gs_tiles[n] = gs
-            for h in range(2):
+            for h in (1, 0):
                 nc.scalar.activation(
                     out=gs[:, 512 * h : 512 * (h + 1)], in_=zz_tiles[(n, h)][:], func=ACT.Sigmoid
                 )
@@ -312,39 +317,40 @@ def tile_full_tmix_params_pb_t_kernel(tc, x, v_first, x_v, Wv, v0, xv_v1, v2, ou
             for h in range(2):
                 cs = slice(512 * h, 512 * (h + 1))
                 nc.vector.tensor_tensor(out=d[:, cs], in0=d[:, cs], in1=pp_tiles[(n, h)][:], op=ALU.add)
-            nc.sync.dma_start(out=of[P * n : P * (n + 1), :], in_=d[:])
+                nc.sync.dma_start(out=of[P * n : P * (n + 1), cs], in_=d[:, cs])
 
-        for n in range(-10, NT + 1):
+        for n in range(-7, NT + 1):
             if 0 <= n - 1 < NT:
                 fin(n - 1)
-            if (n + 18) % 4 == 0 and 3 <= (n + 18) // 4 < NCHUNK:
-                load_x((n + 18) // 4)
+            if (n + 15) % 4 == 0 and 3 <= (n + 15) // 4 < NCHUNK:
+                load_x((n + 15) // 4, 1)
             if (n + 9) % 4 == 0 and 1 <= (n + 9) // 4 < NCHUNK:
                 load_vf((n + 9) // 4)
+            if 0 <= n + 7 < NT:
+                xtr(n + 7)
+            if 0 <= n + 1 < NT:
+                sig(n + 1)
+            if n == -3:
+                prep_v0()
+            if (n + 3) % 4 == 0 and 0 <= (n + 3) // 4 < NCHUNK:
+                prep_aT((n + 3) // 4)
             if 0 <= n + 1 < NT:
                 mx(n + 1)
-                sig(n + 1)
-            if 0 <= n + 9 < NT:
-                t2ops(n + 9)
-            if 0 <= n + 6 < NT:
-                rg(n + 6)
             if 0 <= n + 2 < NT:
                 zgrp(n + 2)
-            if -8 <= n <= -5:
-                prep_w(n + 8)
-            if 0 <= n + 10 < NT:
-                xtr(n + 10)
-            if 0 <= n + 8 < NT:
-                a2ops(n + 8)
+            if 0 <= n + 4 < NT:
+                rg(n + 4)
+            if 0 <= n + 7 < NT:
+                t2ops(n + 7)
+            if 0 <= n + 6 < NT:
+                a2ops(n + 6)
+            if -6 <= n <= -3:
+                prep_w(n + 6)
+            if n == -4 or n == -2:
+                quant_w((n + 4) // 2)
             if 0 <= n + 1 < NT:
                 v1(n + 1)
-            if 0 <= n + 5 < NT:
-                quanth(n + 5)
-            if n == -5:
-                prep_v0()
-                prep_aT(0)
-            if n == -2:
-                for k in range(1, 4):
-                    prep_aT(k)
+            if 0 <= n + 4 < NT:
+                quanth(n + 4)
             if 0 <= n + 1 < NT:
                 v2op(n + 1)

@@ -328,6 +328,8 @@ def tile_full_tmix_params_pb_t_kernel(tc, x, v_first, x_v, Wv, v0, xv_v1, v2, ou
                 load_vf((n + 9) // 4)
             if 0 <= n + 7 < NT:
                 xtr(n + 7)
+            if 0 <= n + 4 < NT:
+                rg(n + 4)
             if 0 <= n + 1 < NT:
                 sig(n + 1)
             if n == -3:
@@ -338,8 +340,6 @@ def tile_full_tmix_params_pb_t_kernel(tc, x, v_first, x_v, Wv, v0, xv_v1, v2, ou
                 mx(n + 1)
             if 0 <= n + 2 < NT:
                 zgrp(n + 2)
-            if 0 <= n + 4 < NT:
-                rg(n + 4)
             if 0 <= n + 7 < NT:
                 t2ops(n + 7)
             if 0 <= n + 6 < NT:

from contextlib import ExitStack

import concourse.mybir as mybir
from concourse.masks import make_identity

F32 = mybir.dt.float32
BF16 = mybir.dt.bfloat16
U32 = mybir.dt.uint32
U8 = mybir.dt.uint8
FP8X4 = mybir.dt.float8_e4m3fn_x4
ALU = mybir.AluOpType
ACT = mybir.ActivationFunctionType

P = 128
TOK = 4096
C = 1024
DV = 128
CHUNK = 512
NCHUNK = TOK // CHUNK
NT = TOK // P
SEQ_CHUNKS = 1024 // CHUNK
TW = CHUNK + 4
HALF = CHUNK // 2

FLOPS = 2 * TOK * C * C + 2 * TOK * DV * C


def tile_full_tmix_params_pb_t_kernel(tc, x, v_first, x_v, Wv, v0, xv_v1, v2, out):
    nc = tc.nc
    xf = x.flatten_outer_dims()
    vff = v_first.flatten_outer_dims()
    af = xv_v1.flatten_outer_dims()
    of = out.flatten_outer_dims()

    with ExitStack() as ctx:
        ctx.enter_context(tc.manual_schedule())
        const = ctx.enter_context(tc.tile_pool(name="const", bufs=1))
        wpool = ctx.enter_context(tc.tile_pool(name="wpool", bufs=1))
        xpool = ctx.enter_context(tc.tile_pool(name="xpool", bufs=3))
        vpool = ctx.enter_context(tc.tile_pool(name="vpool", bufs=3))
        xvpool = ctx.enter_context(tc.tile_pool(name="xvpool", bufs=3))
        t2pool = ctx.enter_context(tc.tile_pool(name="t2pool", bufs=3))
        gpool = ctx.enter_context(tc.tile_pool(name="gpool", bufs=2))
        cpool = ctx.enter_context(tc.tile_pool(name="cpool", bufs=4))
        spool = ctx.enter_context(tc.tile_pool(name="spool", bufs=3))
        dpool = ctx.enter_context(tc.tile_pool(name="dpool", bufs=5))
        apool = ctx.enter_context(tc.tile_pool(name="apool", bufs=2))
        psA = ctx.enter_context(tc.psum_pool(name="psA", bufs=2))
        psP = ctx.enter_context(tc.psum_pool(name="psP", bufs=4))
        psZ = ctx.enter_context(tc.psum_pool(name="psZ", bufs=2))

        xs_tiles = {}
        vf_tiles = {}
        xt_tiles = {}
        xvp_tiles = {}
        t2_tiles = {}
        grp_tiles = {}
        xc_tiles = {}
        xsc_tiles = {}
        pp_tiles = {}
        zz_tiles = {}
        gs_tiles = {}
        d_tiles = {}
        aT_tiles = {}

        def load_x(ck, pieces):
            xs = xpool.tile([P, 4, C], BF16, name="xs")
            src = xf[CHUNK * ck : CHUNK * (ck + 1), :].rearrange("(t p) c -> p t c", p=P)
            w = C // pieces
            for i in range(pieces):
                nc.sync.dma_start(out=xs[:, :, w * i : w * (i + 1)], in_=src[:, :, w * i : w * (i + 1)])
            xs_tiles[ck] = xs

        def load_vf(ck):
            vt = vpool.tile([P, 4, C], BF16, name="vt")
            nc.sync.dma_start(
                out=vt[:],
                in_=vff[CHUNK * ck : CHUNK * (ck + 1), :].rearrange("(t p) c -> p t c", p=P),
            )
            vf_tiles[ck] = vt

        wrow = const.tile([P, 2 * P], BF16, name="wrow")
        nc.vector.memset(wrow[:], 0.0)
        nc.sync.dma_start(out=wrow[0:4, :], in_=x_v.rearrange("(u q) -> u q", q=2 * P))
        load_x(0, 4)
        wv_sb = wpool.tile([P, 8, C], BF16, name="wv_sb")
        wv_view = Wv.rearrange("(o p) k -> p o k", p=P)
        for q in range(4):
            nc.sync.dma_start(out=wv_sb[:, 2 * q : 2 * q + 2, :], in_=wv_view[:, 2 * q : 2 * q + 2, :])
        a_sb = const.tile([P, NT, DV], BF16, name="a_sb")
        a_view = af.rearrange("(m p) d -> p m d", p=P)
        nc.sync.dma_start(out=a_sb[:, 0:8, :], in_=a_view[:, 0:8, :])
        v0row = const.tile([P, P], BF16, name="v0row")
        nc.vector.memset(v0row[:], 0.0)
        nc.sync.dma_start(out=v0row[0:8, :], in_=v0.rearrange("(o p) -> o p", p=P))
        v0one = const.tile([P, 512], BF16, name="v0one")
        nc.vector.memset(v0one[:], 0.0)
        nc.sync.dma_start(out=v0one[0:1, :], in_=v0.rearrange("(o c) -> o c", c=512)[0:1, :])
        v2_sb = const.tile([P, C], BF16, name="v2_sb")
        nc.sync.dma_start(out=v2_sb[:], in_=v2)
        load_x(1, 1)
        load_vf(0)
        nc.sync.dma_start(out=a_sb[:, 8:NT, :], in_=a_view[:, 8:NT, :])
        load_x(2, 1)

        ident_f = const.tile([P, P], F32, name="ident_f")
        make_identity(nc, ident_f[:])
        ident_b = const.tile([P, P], BF16, name="ident_b")
        make_identity(nc, ident_b[:])
        ones_b = const.tile([P, P], BF16, name="ones_b")
        nc.vector.memset(ones_b[:], 1.0)
        zero4 = const.tile([P, 4], F32, name="zero4")
        nc.vector.memset(zero4[:], 0.0)

        wps = psZ.tile([P, 512], F32, name="wps", tag="zz")
        nc.tensor.transpose(wps[:, 0:P], wrow[:].bitcast(F32), ident_f[:])
        w_col = const.tile([P, 8], F32, name="w_col")
        nc.vector.tensor_copy(out=w_col[:], in_=wps[:].bitcast(BF16)[:, 0:8])
        omw = const.tile([P, 8], F32, name="omw")
        nc.vector.tensor_scalar(
            out=omw[:], in0=w_col[:], scalar1=-1.0, scalar2=1.0, op0=ALU.mult, op1=ALU.add
        )
        v0T = const.tile([P, 4, P], F32, name="v0T")

        def prep_v0():
            v0ps = psZ.tile([P, P], BF16, name="v0ps", tag="zz")
            nc.tensor.transpose(v0ps[:], v0row[:], ident_b[:])
            nc.vector.tensor_copy(out=v0T[:], in_=v0ps[:, 4:8].unsqueeze(2).to_broadcast([P, 4, P]))

        def prep_aT(ck):
            aps = psZ.tile([P, CHUNK], BF16, name="aps", tag="zz")
            for m in range(4):
                nc.tensor.transpose(aps[:, P * m : P * (m + 1)], a_sb[:, 4 * ck + m, :], ident_b[:])
            aT = apool.tile([P, CHUNK], BF16, name="aT")
            nc.scalar.copy(out=aT[:], in_=aps[:])
            aT_tiles[ck] = aT

        w_codes = const.tile([P, 2, C], U32, name="w_codes", align_bytes=64)
        w_scales = const.tile([P, 2, C], U8, name="w_scales", align_bytes=64)
        wg0 = wpool.tile([P, 4 * C], BF16, name="wg0", align_bytes=64)
        wg1 = wpool.tile([P, 4 * C], BF16, name="wg1", align_bytes=64)
        wgs = [wg0, wg1]

        def prep_w(q):
            for g in range(2):
                wt = psP.tile([P, 2, 256], F32, name="wt", tag="pp")
                for u in range(2):
                    for oo in range(2):
                        i = 2 * g + u
                        nc.tensor.transpose(
                            wt[:, u, P * oo : P * (oo + 1)],
                            wv_sb[:, 2 * q + oo, :].bitcast(F32)[:, P * i : P * (i + 1)],
                            ident_f[:],
                        )
                w_dst = wgs[g][:, 1024 * q : 1024 * (q + 1)].bitcast(F32).rearrange("p (c u) -> p c u", u=2)
                if g == 0:
                    nc.vector.tensor_copy(out=w_dst, in_=wt[:].rearrange("p u c -> p c u"))
                else:
                    nc.scalar.copy(out=w_dst, in_=wt[:].rearrange("p u c -> p c u"))

        def quant_w(h):
            if True:
                for g in range(2):
                    nc.vector.quantize_mx(
                        out=w_codes[:, g, 512 * h : 512 * (h + 1)].bitcast(FP8X4),
                        scales=w_scales[:, g, 512 * h : 512 * (h + 1)],
                        in_=wgs[g][:, 2048 * h : 2048 * (h + 1)],
                    )

        def xtr(a):
            ck, i = divmod(a, 4)
            xs = xs_tiles[ck]
            xt = psA.tile([P, CHUNK], F32, name="xt")
            for tt in range(4):
                nc.tensor.transpose(
                    xt[:, P * tt : P * (tt + 1)],
                    xs[:, tt, :].bitcast(F32)[:, P * i : P * (i + 1)],
                    ident_f[:],
                )
            xt_tiles[a] = xt

        def t2ops(a):
            ck, i = divmod(a, 4)
            g, u = divmod(i, 2)
            if u == 0:
                t2 = t2pool.tile([P, 4, TW], F32, name="t2")
                t2_tiles[(ck, g)] = t2
                if ck % SEQ_CHUNKS == 0:
                    nc.scalar.copy(out=t2[:, :, 0:1], in_=zero4[:].unsqueeze(2))
                else:
                    nc.scalar.copy(
                        out=t2[:, :, 0:1], in_=t2_tiles[(ck - 1, g)][:, :, CHUNK : CHUNK + 1]
                    )
            t2 = t2_tiles[(ck, g)]
            xb = xt_tiles[a][:].bitcast(BF16).rearrange("p (t e) -> p t e", e=2)
            for e in range(2):
                j = 2 * u + e
                pl = 4 * g + j
                nc.scalar.activation(
                    out=t2[:, j, 1 : CHUNK + 1], in_=xb[:, :, e], func=ACT.Copy, scale=w_col[:, pl : pl + 1]
                )

        def a2ops(a):
            ck, i = divmod(a, 4)
            g, u = divmod(i, 2)
            if u == 0:
                xvp = xvpool.tile([P, 4, CHUNK], BF16, name="xvp")
                xvp_tiles[(ck, g)] = xvp
            xvp = xvp_tiles[(ck, g)]
            t2 = t2_tiles[(ck, g)]
            xb = xt_tiles[a][:].bitcast(BF16).rearrange("p (t e) -> p t e", e=2)
            for e in range(2):
                j = 2 * u + e
                pl = 4 * g + j
                nc.vector.scalar_tensor_tensor(
                    out=xvp[:, j, :],
                    in0=xb[:, :, e],
                    scalar=omw[:, pl : pl + 1],
                    in1=t2[:, j, 0:CHUNK],
                    op0=ALU.mult,
                    op1=ALU.add,
                )

        def rg(r):
            ck, rr = divmod(r, 4)
            g, hh = divmod(rr, 2)
            if hh == 0:
                grp = gpool.tile([P, CHUNK, 4], BF16, name="grp", align_bytes=64)
                grp_tiles[(ck, g)] = grp
            grp = grp_tiles[(ck, g)]
            xvp = xvp_tiles[(ck, g)]
            lo = HALF * hh
            nc.scalar.copy(
                out=grp[:, lo : lo + HALF, :].rearrange("p (c i) j -> p c j i", i=4),
                in_=xvp[:, :, lo : lo + HALF].rearrange("p j (c i) -> p c j i", i=4),
            )

        def quanth(r):
            ck, rr = divmod(r, 4)
            g, hh = divmod(rr, 2)
            if hh == 0:
                xc = cpool.tile([P, CHUNK], U32, name="xc", align_bytes=64)
                xsc = cpool.tile([P, CHUNK], U8, name="xsc", align_bytes=64)
                xc_tiles[(ck, g)] = xc
                xsc_tiles[(ck, g)] = xsc
            lo = HALF * hh
            nc.vector.quantize_mx(
                out=xc_tiles[(ck, g)][:, lo : lo + HALF].bitcast(FP8X4),
                scales=xsc_tiles[(ck, g)][:, lo : lo + HALF],
                in_=grp_tiles[(ck, g)][:, lo : lo + HALF, :].rearrange("p t j -> p (t j)"),
            )

        def mx(n):
            ck, tt = divmod(n, 4)
            ts = slice(P * tt, P * (tt + 1))
            for h in range(2):
                cs = slice(512 * h, 512 * (h + 1))
                pp = psP.tile([P, 512], F32, name="pp")
                pp_tiles[(n, h)] = pp
                for g in range(2):
                    nc.tensor.matmul_mx(
                        out=pp[:],
                        lhsT=xc_tiles[(ck, g)][:, ts].bitcast(FP8X4),
                        lhsT_scale=xsc_tiles[(ck, g)][:, ts],
                        rhs=w_codes[:, g, cs].bitcast(FP8X4),
                        rhs_scale=w_scales[:, g, cs],
                        start=(g == 0),
                        stop=(g == 1),
                    )

        def zgrp(n):
            ck, tt = divmod(n, 4)
            for h in (1, 0):
                cs = slice(512 * h, 512 * (h + 1))
                zz = psZ.tile([P, 512], F32, name="zz")
                zz_tiles[(n, h)] = zz
                if h == 0:
                    nc.tensor.matmul(out=zz[:], lhsT=ones_b[:], rhs=v0one[:], start=True, stop=False)
                else:
                    for i in range(4):
                        nc.tensor.matmul(
                            out=zz[:, P * i : P * (i + 1)],
                            lhsT=v0T[:, i, :],
                            rhs=ident_f[:],
                            is_transpose=True,
                            start=(i == 0),
                            stop=False,
                        )
                nc.tensor.matmul(
                    out=zz[:], lhsT=aT_tiles[ck][:, P * tt : P * (tt + 1)], rhs=v2_sb[:, cs], start=False, stop=True
                )

        def sig(n):
            gs = spool.tile([P, C], F32, name="gs")
            gs_tiles[n] = gs
            for h in (1, 0):
                nc.scalar.activation(
                    out=gs[:, 512 * h : 512 * (h + 1)], in_=zz_tiles[(n, h)][:], func=ACT.Sigmoid
                )

        def v1(n):
            ck, tt = divmod(n, 4)
            d = dpool.tile([P, C], F32, name="d")
            d_tiles[n] = d
            for h in range(2):
                cs = slice(512 * h, 512 * (h + 1))
                nc.vector.tensor_tensor(
                    out=d[:, cs], in0=vf_tiles[ck][:, tt, cs], in1=pp_tiles[(n, h)][:], op=ALU.subtract
                )

        def v2op(n):
            d = d_tiles[n]
            nc.gpsimd.tensor_tensor(out=d[:], in0=d[:], in1=gs_tiles[n][:], op=ALU.mult)

        def fin(n):
            d = d_tiles[n]
            for h in range(2):
                cs = slice(512 * h, 512 * (h + 1))
                nc.vector.tensor_tensor(out=d[:, cs], in0=d[:, cs], in1=pp_tiles[(n, h)][:], op=ALU.add)
                nc.sync.dma_start(out=of[P * n : P * (n + 1), cs], in_=d[:, cs])

        for n in range(-7, NT + 1):
            if 0 <= n - 1 < NT:
                fin(n - 1)
            if (n + 15) % 4 == 0 and 3 <= (n + 15) // 4 < NCHUNK:
                load_x((n + 15) // 4, 1)
            if (n + 9) % 4 == 0 and 1 <= (n + 9) // 4 < NCHUNK:
                load_vf((n + 9) // 4)
            if 0 <= n + 7 < NT:
                xtr(n + 7)
            if 0 <= n + 4 < NT:
                rg(n + 4)
            if 0 <= n + 1 < NT:
                sig(n + 1)
            if n == -3:
                prep_v0()
            if (n + 3) % 4 == 0 and 0 <= (n + 3) // 4 < NCHUNK:
                prep_aT((n + 3) // 4)
            if 0 <= n + 1 < NT:
                mx(n + 1)
            if 0 <= n + 2 < NT:
                zgrp(n + 2)
            if 0 <= n + 7 < NT:
                t2ops(n + 7)
            if 0 <= n + 6 < NT:
                a2ops(n + 6)
            if -6 <= n <= -3:
                prep_w(n + 6)
            if n == -4 or n == -2:
                quant_w((n + 4) // 2)
            if 0 <= n + 1 < NT:
                v1(n + 1)
            if 0 <= n + 4 < NT:
                quanth(n + 4)
            if 0 <= n + 1 < NT:
                v2op(n + 1)
